import numpy as np
import ml_dtypes


def mxq(x, axis, fmt="e4m3"):
    dtype, down = {"e4m3": (ml_dtypes.float8_e4m3fn, 7), "e5m2": (ml_dtypes.float8_e5m2, 14)}[fmt]
    v = np.moveaxis(np.asarray(x, np.float32).astype(ml_dtypes.bfloat16).astype(np.float64), axis, -1)
    blocks = v.reshape(v.shape[:-1] + (-1, 32))
    amax = np.abs(blocks).max(-1, keepdims=True)
    byte = np.maximum(np.where(amax > 0, np.frexp(amax)[1] - 1 + 127, 0) - down, 1)
    scale = np.exp2(byte - 127.0)
    codes = (blocks / scale).astype(np.float32).astype(dtype).astype(np.float64)
    return np.moveaxis((codes * scale).reshape(v.shape), -1, axis)


WIDE = False


def mx_kscale(k):
    if not WIDE:
        return np.ones(k)
    levels = np.array([10, -10, 5, -5, 0])
    a = np.random.permutation(np.resize(levels, k // 512 * 4)).reshape(k // 512, 4)
    idx = np.arange(k)
    return np.exp2(a[idx // 512, idx % 128 // 32])


BF16 = ml_dtypes.bfloat16


def bf(x):
    return np.asarray(x, np.float32).astype(BF16)


def f64(x):
    return np.asarray(x).astype(np.float64)


B, S, D, A0, A1, A2 = 2, 128, 4096, 64, 32, 128
AM = min(A0, A1, A2)


def kron(a, b):
    return (a[:, None, :, None] * b[None, :, None, :]).reshape(a.shape[0] * b.shape[0], a.shape[1] * b.shape[1])


def setup_inputs():
    u = mx_kscale(D)[:: D // AM]
    s = np.repeat(u, D // AM)
    inp = {"x": bf(np.random.standard_normal((B, S, D)) * s)}
    for i, a in enumerate((A0, A1, A2)):
        inp[f"L{i}"] = bf(np.random.uniform(size=(a, a)) / np.repeat(u, a // AM)[:, None])
        inp[f"R{i}"] = bf(np.random.uniform(size=(D // a, D // a)) * 3.0 / np.sqrt(D))
    inp["bias"] = bf(np.random.uniform(size=D))
    return inp


def reference(x, L0, R0, L1, R1, L2, R2, bias):
    pairs = [(f64(L0), f64(R0)), (f64(L1), f64(R1)), (f64(L2), f64(R2))]
    W = kron(pairs[0][0], pairs[0][1])
    for l, r in pairs[1:]:
        W = W + kron(l, r)
    W = W / len(pairs)
    return (mxq(f64(x), 2, "e4m3") @ mxq(W, 0, "e4m3")) + f64(bias)

@@ -1,0 +1,197 @@
+from contextlib import ExitStack
+
+import concourse.mybir as mybir
+from concourse.masks import make_identity
+
+F32 = mybir.dt.float32
+BF16 = mybir.dt.bfloat16
+U32 = mybir.dt.uint32
+U8 = mybir.dt.uint8
+FP8X4 = mybir.dt.float8_e4m3fn_x4
+MULT = mybir.AluOpType.mult
+ADD = mybir.AluOpType.add
+COPY = mybir.ActivationFunctionType.Copy
+
+P = 128
+D = 4096
+TOKENS = 256
+TOKEN_TILES = TOKENS // P
+PACK = 4
+PASSES = D // (P * PACK)
+B = 32
+ROW = PASSES * B * PACK
+RUN = B * PACK
+D_STEP = 4
+SLOTS = 2 * D_STEP
+BLOCK_COLS = SLOTS * B
+QUANT_IN = 4096
+
+R2_AT = 0
+R0_AT = 32
+R1_AT = 96
+R_COLS = 224
+
+FLOPS = 2 * TOKENS * D * D
+
+
+def tile_klinear_kernel(tc, x, L0, R0, L1, R1, L2, R2, bias, out):
+    nc = tc.nc
+    x_rows = x.flatten_outer_dims()
+    out_rows = out.flatten_outer_dims()
+
+    with ExitStack() as pools:
+        keep = pools.enter_context(tc.tile_pool(name="keep", bufs=1))
+        stage = pools.enter_context(tc.tile_pool(name="stage", bufs=1))
+        sums = pools.enter_context(tc.tile_pool(name="sums", bufs=4))
+        blocks = pools.enter_context(tc.tile_pool(name="blocks", bufs=2))
+        xt_pool = pools.enter_context(tc.psum_pool(name="xt", bufs=2))
+        acc_pool = pools.enter_context(tc.psum_pool(name="acc", bufs=2))
+
+        r_raw = stage.tile([P, R_COLS], BF16)
+        for rep in range(4):
+            nc.sync.dma_start(out=r_raw[32 * rep : 32 * rep + 32, R2_AT : R2_AT + 32], in_=R2[:, :])
+        l2_raw = stage.tile([P, 32, 128], BF16)
+        for rep in range(4):
+            nc.sync.dma_start(
+                out=l2_raw[32 * rep : 32 * rep + 32],
+                in_=L2.rearrange("(a h) n -> h a n", h=4)[rep : rep + 1].to_broadcast([32, 32, 128]),
+            )
+        for rep in range(2):
+            nc.sync.dma_start(out=r_raw[64 * rep : 64 * rep + 64, R0_AT : R0_AT + 64], in_=R0[:, :])
+        l0_raw = stage.tile([P, 32, 64], BF16)
+        for rep in range(2):
+            nc.sync.dma_start(
+                out=l0_raw[64 * rep : 64 * rep + 64],
+                in_=L0.rearrange("(a h) n -> h a n", h=2)[rep : rep + 1].to_broadcast([64, 32, 64]),
+            )
+        nc.sync.dma_start(out=r_raw[:, R1_AT : R1_AT + 128], in_=R1[:, :])
+        l1_raw = stage.tile([P, 32, 32], BF16)
+        nc.sync.dma_start(
+            out=l1_raw[:].rearrange("p a n -> p (a n)"),
+            in_=L1.rearrange("a n -> (a n)").partition_broadcast(P),
+        )
+        r_third = keep.tile([P, R_COLS], F32)
+        nc.vector.tensor_scalar_mul(out=r_third[:], in0=r_raw[:], scalar1=1.0 / 3.0)
+
+        l2_rows = keep.tile([P, 2, 2, ROW], BF16)
+        l2_view = l2_raw[:].rearrange("p (c t) (b f g) -> p g f c b t", t=PACK, f=2, g=2)
+        for g in range(2):
+            for f in range(2):
+                nc.vector.tensor_copy(
+                    out=l2_rows[:, g, f, :].rearrange("p (c b t) -> p c b t", c=PASSES, b=B),
+                    in_=l2_view[:, g, f],
+                )
+        l0_rows = keep.tile([P, 2, ROW], BF16)
+        l0_view = l0_raw[:].rearrange("p (c t) (b f) -> p f c b t", t=PACK, f=2)
+        for f in range(2):
+            nc.vector.tensor_copy(
+                out=l0_rows[:, f, :].rearrange("p (c b t) -> p c b t", c=PASSES, b=B),
+                in_=l0_view[:, f],
+            )
+        l1_rows = keep.tile([P, ROW], BF16)
+        nc.vector.tensor_copy(
+            out=l1_rows[:].rearrange("p (c b t) -> p c b t", c=PASSES, b=B),
+            in_=l1_raw[:].rearrange("p (c t) b -> p c b t", t=PACK),
+        )
+        l1_by_pass = l1_rows[:].rearrange("p (c j) -> p c j", c=PASSES)
+
+        x_sb = stage.tile([P, TOKEN_TILES, D], BF16)
+        for m in range(TOKEN_TILES):
+            nc.scalar.dma_start(out=x_sb[:, m, :], in_=x_rows[m * P : (m + 1) * P, :])
+        bias_all = keep.tile([P, D], BF16)
+        nc.scalar.dma_start(out=bias_all[:], in_=bias.partition_broadcast(P))
+
+        x_codes = keep.tile([P, PASSES * TOKENS], U32, align_bytes=64)
+        x_scales = keep.tile([P, PASSES * TOKENS], U8, align_bytes=64)
+        result = keep.tile([P, TOKEN_TILES, D], F32)
+
+        def prepare_x():
+            ident = keep.tile([P, P], BF16)
+            make_identity(nc, ident[:])
+            x_grouped = stage.tile([P, PASSES, TOKENS * PACK], BF16, align_bytes=64)
+            for c in range(PASSES):
+                x_t = xt_pool.tile([P, TOKEN_TILES, PACK, P], BF16)
+                for m in range(TOKEN_TILES):
+                    for t in range(PACK):
+                        k0 = (c * PACK + t) * P
+                        nc.tensor.transpose(x_t[:, m, t, :], x_sb[:, m, k0 : k0 + P], ident[:])
+                nc.scalar.copy(
+                    out=x_grouped[:, c, :].rearrange("p (m r t) -> p m r t", m=TOKEN_TILES, t=PACK),
+                    in_=x_t[:].rearrange("p m t r -> p m r t"),
+                )
+            x_flat = x_grouped[:].rearrange("p c j -> p (c j)")
+            for h in range(PASSES * TOKENS * PACK // QUANT_IN):
+                words = slice(h * QUANT_IN // PACK, (h + 1) * QUANT_IN // PACK)
+                nc.vector.quantize_mx(
+                    out=x_codes[:, words].bitcast(FP8X4),
+                    scales=x_scales[:, words],
+                    in_=x_flat[:, h * QUANT_IN : (h + 1) * QUANT_IN],
+                )
+
+        def build_block(q, g):
+            w_bf16 = blocks.tile([P, PASSES, SLOTS, RUN], BF16, align_bytes=64)
+            for e in range(D_STEP):
+                d = D_STEP * q + e
+                r2 = r_third[:, R2_AT + d : R2_AT + d + 1]
+                r0 = r_third[:, R0_AT + 32 * g + d : R0_AT + 32 * g + d + 1]
+                partial = sums.tile([P, 2, ROW], F32)
+                nc.scalar.activation(out=partial[:], in_=l2_rows[:, g], func=COPY, scale=r2)
+                nc.vector.scalar_tensor_tensor(
+                    out=partial[:], in0=l0_rows[:], scalar=r0, in1=partial[:], op0=MULT, op1=ADD
+                )
+                for f in range(2):
+                    r1_at = R1_AT + 64 * f + 32 * g + d
+                    nc.vector.scalar_tensor_tensor(
+                        out=w_bf16[:, :, D_STEP * f + e, :],
+                        in0=l1_by_pass,
+                        scalar=r_third[:, r1_at : r1_at + 1],
+                        in1=partial[:, f, :].rearrange("p (c j) -> p c j", c=PASSES),
+                        op0=MULT,
+                        op1=ADD,
+                    )
+            w_codes = blocks.tile([P, PASSES * BLOCK_COLS], U32, align_bytes=64)
+            w_scales = blocks.tile([P, PASSES * BLOCK_COLS], U8, align_bytes=64)
+            w_flat = w_bf16[:].rearrange("p c s j -> p (c s j)")
+            for h in range(PASSES * BLOCK_COLS * PACK // QUANT_IN):
+                words = slice(h * QUANT_IN // PACK, (h + 1) * QUANT_IN // PACK)
+                nc.vector.quantize_mx(
+                    out=w_codes[:, words].bitcast(FP8X4),
+                    scales=w_scales[:, words],
+                    in_=w_flat[:, h * QUANT_IN : (h + 1) * QUANT_IN],
+                )
+            return w_codes, w_scales
+
+        def multiply_block(q, g, w_codes, w_scales):
+            acc = [acc_pool.tile([P, BLOCK_COLS], F32, name="acc%d" % m) for m in range(TOKEN_TILES)]
+            for c in range(PASSES):
+                w_cols = slice(c * BLOCK_COLS, (c + 1) * BLOCK_COLS)
+                for m in range(TOKEN_TILES):
+                    x_cols = slice(c * TOKENS + m * P, c * TOKENS + (m + 1) * P)
+                    nc.tensor.matmul_mx(
+                        out=acc[m][:],
+                        lhsT=x_codes[:, x_cols].bitcast(FP8X4),
+                        lhsT_scale=x_scales[:, x_cols],
+                        rhs=w_codes[:, w_cols].bitcast(FP8X4),
+                        rhs_scale=w_scales[:, w_cols],
+                        start=(c == 0),
+                        stop=(c == PASSES - 1),
+                    )
+            by_n = "p (b f g q e) -> p g q b f e"
+            for m in range(TOKEN_TILES):
+                nc.vector.tensor_tensor(
+                    out=result[:, m, :].rearrange(by_n, b=B, f=2, g=2, e=D_STEP)[:, g, q],
+                    in0=acc[m][:].rearrange("p (f e b) -> p b f e", f=2, e=D_STEP),
+                    in1=bias_all[:].rearrange(by_n, b=B, f=2, g=2, e=D_STEP)[:, g, q],
+                    op=ADD,
+                )
+
+        block_list = [(q, g) for q in range(32 // D_STEP) for g in range(2)]
+        first = build_block(*block_list[0])
+        prepare_x()
+        multiply_block(*block_list[0], *first)
+        for q, g in block_list[1:]:
+            w_codes, w_scales = build_block(q, g)
+            multiply_block(q, g, w_codes, w_scales)
+
+        for m in range(TOKEN_TILES):
+            nc.sync.dma_start(out=out_rows[m * P : (m + 1) * P, :], in_=result[:, m, :])

@@ -25,6 +25,8 @@ D_STEP = 4
 SLOTS = 2 * D_STEP
 BLOCK_COLS = SLOTS * B
 QUANT_IN = 4096
+MATMUL_COLS = 512
+VECTOR_UNITS_OF_8 = 3
 
 R2_AT = 0
 R0_AT = 32
@@ -42,72 +44,79 @@ def tile_klinear_kernel(tc, x, L0, R0, L1, R1, L2, R2, bias, out):
     with ExitStack() as pools:
         keep = pools.enter_context(tc.tile_pool(name="keep", bufs=1))
         stage = pools.enter_context(tc.tile_pool(name="stage", bufs=1))
-        sums = pools.enter_context(tc.tile_pool(name="sums", bufs=4))
+        partials = pools.enter_context(tc.tile_pool(name="partials", bufs=5))
+        products = pools.enter_context(tc.tile_pool(name="products", bufs=3))
         blocks = pools.enter_context(tc.tile_pool(name="blocks", bufs=2))
-        xt_pool = pools.enter_context(tc.psum_pool(name="xt", bufs=2))
+        l_psum = pools.enter_context(tc.psum_pool(name="l_psum", bufs=1))
+        xt_pool = pools.enter_context(tc.psum_pool(name="xt", bufs=1))
         acc_pool = pools.enter_context(tc.psum_pool(name="acc", bufs=2))
+
+        ident = keep.tile([P, P], BF16)
+        make_identity(nc, ident[:])
 
         r_raw = stage.tile([P, R_COLS], BF16)
         for rep in range(4):
-            nc.sync.dma_start(out=r_raw[32 * rep : 32 * rep + 32, R2_AT : R2_AT + 32], in_=R2[:, :])
+            nc.scalar.dma_start(out=r_raw[32 * rep : 32 * rep + 32, R2_AT : R2_AT + 32], in_=R2[:, :])
+        for rep in range(2):
+            nc.scalar.dma_start(out=r_raw[64 * rep : 64 * rep + 64, R0_AT : R0_AT + 64], in_=R0[:, :])
+        nc.scalar.dma_start(out=r_raw[:, R1_AT : R1_AT + 128], in_=R1[:, :])
         l2_raw = stage.tile([P, 32, 128], BF16)
         for rep in range(4):
             nc.sync.dma_start(
                 out=l2_raw[32 * rep : 32 * rep + 32],
                 in_=L2.rearrange("(a h) n -> h a n", h=4)[rep : rep + 1].to_broadcast([32, 32, 128]),
             )
-        for rep in range(2):
-            nc.sync.dma_start(out=r_raw[64 * rep : 64 * rep + 64, R0_AT : R0_AT + 64], in_=R0[:, :])
         l0_raw = stage.tile([P, 32, 64], BF16)
         for rep in range(2):
             nc.sync.dma_start(
                 out=l0_raw[64 * rep : 64 * rep + 64],
                 in_=L0.rearrange("(a h) n -> h a n", h=2)[rep : rep + 1].to_broadcast([64, 32, 64]),
             )
-        nc.sync.dma_start(out=r_raw[:, R1_AT : R1_AT + 128], in_=R1[:, :])
         l1_raw = stage.tile([P, 32, 32], BF16)
         nc.sync.dma_start(
             out=l1_raw[:].rearrange("p a n -> p (a n)"),
             in_=L1.rearrange("a n -> (a n)").partition_broadcast(P),
         )
+        x_sb = stage.tile([P, TOKEN_TILES, D], BF16)
+        for m in range(TOKEN_TILES):
+            nc.sync.dma_start(out=x_sb[:, m, :], in_=x_rows[m * P : (m + 1) * P, :])
+        bias_all = keep.tile([P, D], BF16)
+        nc.sync.dma_start(out=bias_all[:], in_=bias.partition_broadcast(P))
+
         r_third = keep.tile([P, R_COLS], F32)
         nc.vector.tensor_scalar_mul(out=r_third[:], in0=r_raw[:], scalar1=1.0 / 3.0)
 
+        def by_cbt(row):
+            return row.rearrange("p (c b t) -> p c b t", c=PASSES, b=B)
+
+        def to_psum(row, name):
+            bank = l_psum.tile([P, ROW], BF16, name=name)
+            for h in range(ROW // MATMUL_COLS):
+                cols = slice(h * MATMUL_COLS, (h + 1) * MATMUL_COLS)
+                nc.tensor.matmul(out=bank[:, cols], lhsT=ident[:], rhs=row[:, cols], start=True, stop=True)
+            return bank
+
         l2_rows = keep.tile([P, 2, 2, ROW], BF16)
         l2_view = l2_raw[:].rearrange("p (c t) (b f g) -> p g f c b t", t=PACK, f=2, g=2)
-        for g in range(2):
-            for f in range(2):
-                nc.vector.tensor_copy(
-                    out=l2_rows[:, g, f, :].rearrange("p (c b t) -> p c b t", c=PASSES, b=B),
-                    in_=l2_view[:, g, f],
-                )
         l0_rows = keep.tile([P, 2, ROW], BF16)
         l0_view = l0_raw[:].rearrange("p (c t) (b f) -> p f c b t", t=PACK, f=2)
-        for f in range(2):
-            nc.vector.tensor_copy(
-                out=l0_rows[:, f, :].rearrange("p (c b t) -> p c b t", c=PASSES, b=B),
-                in_=l0_view[:, f],
-            )
         l1_rows = keep.tile([P, ROW], BF16)
-        nc.vector.tensor_copy(
-            out=l1_rows[:].rearrange("p (c b t) -> p c b t", c=PASSES, b=B),
-            in_=l1_raw[:].rearrange("p (c t) b -> p c b t", t=PACK),
-        )
-        l1_by_pass = l1_rows[:].rearrange("p (c j) -> p c j", c=PASSES)
-
-        x_sb = stage.tile([P, TOKEN_TILES, D], BF16)
-        for m in range(TOKEN_TILES):
-            nc.scalar.dma_start(out=x_sb[:, m, :], in_=x_rows[m * P : (m + 1) * P, :])
-        bias_all = keep.tile([P, D], BF16)
-        nc.scalar.dma_start(out=bias_all[:], in_=bias.partition_broadcast(P))
+        for f in range(2):
+            nc.vector.tensor_copy(out=by_cbt(l2_rows[:, 0, f, :]), in_=l2_view[:, 0, f])
+        for f in range(2):
+            nc.vector.tensor_copy(out=by_cbt(l0_rows[:, f, :]), in_=l0_view[:, f])
+        nc.vector.tensor_copy(out=by_cbt(l1_rows[:]), in_=l1_raw[:].rearrange("p (c t) b -> p c b t", t=PACK))
+        for f in range(2):
+            nc.vector.tensor_copy(out=by_cbt(l2_rows[:, 1, f, :]), in_=l2_view[:, 1, f])
+        l0_banks = [to_psum(l0_rows[:, f, :], "l0_bank%d" % f) for f in range(2)]
+        l1_bank = to_psum(l1_rows[:], "l1_bank")
+        l1_by_pass = l1_bank[:].rearrange("p (c j) -> p c j", c=PASSES)
 
         x_codes = keep.tile([P, PASSES * TOKENS], U32, align_bytes=64)
         x_scales = keep.tile([P, PASSES * TOKENS], U8, align_bytes=64)
         result = keep.tile([P, TOKEN_TILES, D], F32)
 
         def prepare_x():
-            ident = keep.tile([P, P], BF16)
-            make_identity(nc, ident[:])
             x_grouped = stage.tile([P, PASSES, TOKENS * PACK], BF16, align_bytes=64)
             for c in range(PASSES):
                 x_t = xt_pool.tile([P, TOKEN_TILES, PACK, P], BF16)
@@ -134,11 +143,23 @@ def tile_klinear_kernel(tc, x, L0, R0, L1, R1, L2, R2, bias, out):
                 d = D_STEP * q + e
                 r2 = r_third[:, R2_AT + d : R2_AT + d + 1]
                 r0 = r_third[:, R0_AT + 32 * g + d : R0_AT + 32 * g + d + 1]
-                partial = sums.tile([P, 2, ROW], F32)
+                unit = (2 * q + g) * D_STEP + e
+                partial = partials.tile([P, 2, ROW], F32)
                 nc.scalar.activation(out=partial[:], in_=l2_rows[:, g], func=COPY, scale=r2)
-                nc.vector.scalar_tensor_tensor(
-                    out=partial[:], in0=l0_rows[:], scalar=r0, in1=partial[:], op0=MULT, op1=ADD
-                )
+                if (unit * VECTOR_UNITS_OF_8) % 8 < VECTOR_UNITS_OF_8:
+                    for f in range(2):
+                        nc.vector.scalar_tensor_tensor(
+                            out=partial[:, f, :],
+                            in0=l0_banks[f][:],
+                            scalar=r0,
+                            in1=partial[:, f, :],
+                            op0=MULT,
+                            op1=ADD,
+                        )
+                else:
+                    product = products.tile([P, 2, ROW], F32)
+                    nc.scalar.activation(out=product[:], in_=l0_rows[:], func=COPY, scale=r0)
+                    nc.gpsimd.tensor_tensor(out=partial[:], in0=partial[:], in1=product[:], op=ADD)
                 for f in range(2):
                     r1_at = R1_AT + 64 * f + 32 * g + d
                     nc.vector.scalar_tensor_tensor(

@@ -27,6 +27,7 @@ BLOCK_COLS = SLOTS * B
 QUANT_IN = 4096
 MATMUL_COLS = 512
 VECTOR_UNITS_OF_8 = 3
+GPSIMD_PIECE = 512
 
 R2_AT = 0
 R0_AT = 32
@@ -159,7 +160,13 @@ def tile_klinear_kernel(tc, x, L0, R0, L1, R1, L2, R2, bias, out):
                 else:
                     product = products.tile([P, 2, ROW], F32)
                     nc.scalar.activation(out=product[:], in_=l0_rows[:], func=COPY, scale=r0)
-                    nc.gpsimd.tensor_tensor(out=partial[:], in0=partial[:], in1=product[:], op=ADD)
+                    partial_flat = partial[:].rearrange("p f j -> p (f j)")
+                    product_flat = product[:].rearrange("p f j -> p (f j)")
+                    for piece in range(2 * ROW // GPSIMD_PIECE):
+                        cols = slice(piece * GPSIMD_PIECE, (piece + 1) * GPSIMD_PIECE)
+                        nc.gpsimd.tensor_tensor(
+                            out=partial_flat[:, cols], in0=partial_flat[:, cols], in1=product_flat[:, cols], op=ADD
+                        )
                 for f in range(2):
                     r1_at = R1_AT + 64 * f + 32 * g + d
                     nc.vector.scalar_tensor_tensor(

@@ -26,8 +26,7 @@ SLOTS = 2 * D_STEP
 BLOCK_COLS = SLOTS * B
 QUANT_IN = 4096
 MATMUL_COLS = 512
-VECTOR_UNITS_OF_8 = 3
-GPSIMD_PIECE = 512
+VECTOR_UNITS_OF_8 = 4
 
 R2_AT = 0
 R0_AT = 32
@@ -160,13 +159,7 @@ def tile_klinear_kernel(tc, x, L0, R0, L1, R1, L2, R2, bias, out):
                 else:
                     product = products.tile([P, 2, ROW], F32)
                     nc.scalar.activation(out=product[:], in_=l0_rows[:], func=COPY, scale=r0)
-                    partial_flat = partial[:].rearrange("p f j -> p (f j)")
-                    product_flat = product[:].rearrange("p f j -> p (f j)")
-                    for piece in range(2 * ROW // GPSIMD_PIECE):
-                        cols = slice(piece * GPSIMD_PIECE, (piece + 1) * GPSIMD_PIECE)
-                        nc.gpsimd.tensor_tensor(
-                            out=partial_flat[:, cols], in0=partial_flat[:, cols], in1=product_flat[:, cols], op=ADD
-                        )
+                    nc.gpsimd.tensor_tensor(out=partial[:], in0=partial[:], in1=product[:], op=ADD)
                 for f in range(2):
                     r1_at = R1_AT + 64 * f + 32 * g + d
                     nc.vector.scalar_tensor_tensor(

@@ -22,11 +22,11 @@ B = 32
 ROW = PASSES * B * PACK
 RUN = B * PACK
 D_STEP = 4
-SLOTS = 2 * D_STEP
+SLOTS = 4 * D_STEP
 BLOCK_COLS = SLOTS * B
 QUANT_IN = 4096
 MATMUL_COLS = 512
-VECTOR_UNITS_OF_8 = 4
+VECTOR_UNITS_OF_8 = 3
 
 R2_AT = 0
 R0_AT = 32
@@ -46,7 +46,7 @@ def tile_klinear_kernel(tc, x, L0, R0, L1, R1, L2, R2, bias, out):
         stage = pools.enter_context(tc.tile_pool(name="stage", bufs=1))
         partials = pools.enter_context(tc.tile_pool(name="partials", bufs=5))
         products = pools.enter_context(tc.tile_pool(name="products", bufs=3))
-        blocks = pools.enter_context(tc.tile_pool(name="blocks", bufs=2))
+        blocks = pools.enter_context(tc.tile_pool(name="blocks", bufs=1))
         l_psum = pools.enter_context(tc.psum_pool(name="l_psum", bufs=1))
         xt_pool = pools.enter_context(tc.psum_pool(name="xt", bufs=1))
         acc_pool = pools.enter_context(tc.psum_pool(name="acc", bufs=2))
@@ -137,39 +137,43 @@ def tile_klinear_kernel(tc, x, L0, R0, L1, R1, L2, R2, bias, out):
                     in_=x_flat[:, h * QUANT_IN : (h + 1) * QUANT_IN],
                 )
 
-        def build_block(q, g):
-            w_bf16 = blocks.tile([P, PASSES, SLOTS, RUN], BF16, align_bytes=64)
-            for e in range(D_STEP):
-                d = D_STEP * q + e
-                r2 = r_third[:, R2_AT + d : R2_AT + d + 1]
-                r0 = r_third[:, R0_AT + 32 * g + d : R0_AT + 32 * g + d + 1]
-                unit = (2 * q + g) * D_STEP + e
-                partial = partials.tile([P, 2, ROW], F32)
-                nc.scalar.activation(out=partial[:], in_=l2_rows[:, g], func=COPY, scale=r2)
-                if (unit * VECTOR_UNITS_OF_8) % 8 < VECTOR_UNITS_OF_8:
-                    for f in range(2):
-                        nc.vector.scalar_tensor_tensor(
-                            out=partial[:, f, :],
-                            in0=l0_banks[f][:],
-                            scalar=r0,
-                            in1=partial[:, f, :],
-                            op0=MULT,
-                            op1=ADD,
-                        )
-                else:
-                    product = products.tile([P, 2, ROW], F32)
-                    nc.scalar.activation(out=product[:], in_=l0_rows[:], func=COPY, scale=r0)
-                    nc.gpsimd.tensor_tensor(out=partial[:], in0=partial[:], in1=product[:], op=ADD)
+        def build_unit(w_bf16, q, e, g):
+            d = D_STEP * q + e
+            unit = 2 * d + g
+            r2 = r_third[:, R2_AT + d : R2_AT + d + 1]
+            r0 = r_third[:, R0_AT + 32 * g + d : R0_AT + 32 * g + d + 1]
+            partial = partials.tile([P, 2, ROW], F32)
+            nc.scalar.activation(out=partial[:], in_=l2_rows[:, g], func=COPY, scale=r2)
+            if (unit * VECTOR_UNITS_OF_8) % 8 < VECTOR_UNITS_OF_8:
                 for f in range(2):
-                    r1_at = R1_AT + 64 * f + 32 * g + d
                     nc.vector.scalar_tensor_tensor(
-                        out=w_bf16[:, :, D_STEP * f + e, :],
-                        in0=l1_by_pass,
-                        scalar=r_third[:, r1_at : r1_at + 1],
-                        in1=partial[:, f, :].rearrange("p (c j) -> p c j", c=PASSES),
+                        out=partial[:, f, :],
+                        in0=l0_banks[f][:],
+                        scalar=r0,
+                        in1=partial[:, f, :],
                         op0=MULT,
                         op1=ADD,
                     )
+            else:
+                product = products.tile([P, 2, ROW], F32)
+                nc.scalar.activation(out=product[:], in_=l0_rows[:], func=COPY, scale=r0)
+                nc.gpsimd.tensor_tensor(out=partial[:], in0=partial[:], in1=product[:], op=ADD)
+            for f in range(2):
+                r1_at = R1_AT + 64 * f + 32 * g + d
+                nc.vector.scalar_tensor_tensor(
+                    out=w_bf16[:, :, (2 * f + g) * D_STEP + e, :],
+                    in0=l1_by_pass,
+                    scalar=r_third[:, r1_at : r1_at + 1],
+                    in1=partial[:, f, :].rearrange("p (c j) -> p c j", c=PASSES),
+                    op0=MULT,
+                    op1=ADD,
+                )
+
+        def build_block(q):
+            w_bf16 = blocks.tile([P, PASSES, SLOTS, RUN], BF16, align_bytes=64)
+            for e in range(D_STEP):
+                for g in range(2):
+                    build_unit(w_bf16, q, e, g)
             w_codes = blocks.tile([P, PASSES * BLOCK_COLS], U32, align_bytes=64)
             w_scales = blocks.tile([P, PASSES * BLOCK_COLS], U8, align_bytes=64)
             w_flat = w_bf16[:].rearrange("p c s j -> p (c s j)")
@@ -182,7 +186,7 @@ def tile_klinear_kernel(tc, x, L0, R0, L1, R1, L2, R2, bias, out):
                 )
             return w_codes, w_scales
 
-        def multiply_block(q, g, w_codes, w_scales):
+        def multiply_block(q, w_codes, w_scales):
             acc = [acc_pool.tile([P, BLOCK_COLS], F32, name="acc%d" % m) for m in range(TOKEN_TILES)]
             for c in range(PASSES):
                 w_cols = slice(c * BLOCK_COLS, (c + 1) * BLOCK_COLS)
@@ -197,22 +201,21 @@ def tile_klinear_kernel(tc, x, L0, R0, L1, R1, L2, R2, bias, out):
                         start=(c == 0),
                         stop=(c == PASSES - 1),
                     )
-            by_n = "p (b f g q e) -> p g q b f e"
+            by_n = "p (b s q e) -> p q b s e"
             for m in range(TOKEN_TILES):
                 nc.vector.tensor_tensor(
-                    out=result[:, m, :].rearrange(by_n, b=B, f=2, g=2, e=D_STEP)[:, g, q],
-                    in0=acc[m][:].rearrange("p (f e b) -> p b f e", f=2, e=D_STEP),
-                    in1=bias_all[:].rearrange(by_n, b=B, f=2, g=2, e=D_STEP)[:, g, q],
+                    out=result[:, m, :].rearrange(by_n, b=B, s=4, e=D_STEP)[:, q],
+                    in0=acc[m][:].rearrange("p (s e b) -> p b s e", s=4, e=D_STEP),
+                    in1=bias_all[:].rearrange(by_n, b=B, s=4, e=D_STEP)[:, q],
                     op=ADD,
                 )
 
-        block_list = [(q, g) for q in range(32 // D_STEP) for g in range(2)]
-        first = build_block(*block_list[0])
+        first = build_block(0)
         prepare_x()
-        multiply_block(*block_list[0], *first)
-        for q, g in block_list[1:]:
-            w_codes, w_scales = build_block(q, g)
-            multiply_block(q, g, w_codes, w_scales)
+        multiply_block(0, *first)
+        for q in range(1, 32 // D_STEP):
+            w_codes, w_scales = build_block(q)
+            multiply_block(q, w_codes, w_scales)
 
         for m in range(TOKEN_TILES):
             nc.sync.dma_start(out=out_rows[m * P : (m + 1) * P, :], in_=result[:, m, :])

@@ -26,7 +26,9 @@ SLOTS = 4 * D_STEP
 BLOCK_COLS = SLOTS * B
 QUANT_IN = 4096
 MATMUL_COLS = 512
-VECTOR_UNITS_OF_8 = 3
+PARTIAL_BUFS = 8
+PRODUCT_BUFS = 4
+VECTOR_UNITS_OF_8 = 2
 
 R2_AT = 0
 R0_AT = 32
@@ -43,80 +45,79 @@ def tile_klinear_kernel(tc, x, L0, R0, L1, R1, L2, R2, bias, out):
 
     with ExitStack() as pools:
         keep = pools.enter_context(tc.tile_pool(name="keep", bufs=1))
-        stage = pools.enter_context(tc.tile_pool(name="stage", bufs=1))
-        partials = pools.enter_context(tc.tile_pool(name="partials", bufs=5))
-        products = pools.enter_context(tc.tile_pool(name="products", bufs=3))
+        partials = pools.enter_context(tc.tile_pool(name="partials", bufs=PARTIAL_BUFS))
+        products = pools.enter_context(tc.tile_pool(name="products", bufs=PRODUCT_BUFS))
         blocks = pools.enter_context(tc.tile_pool(name="blocks", bufs=1))
         l_psum = pools.enter_context(tc.psum_pool(name="l_psum", bufs=1))
         xt_pool = pools.enter_context(tc.psum_pool(name="xt", bufs=1))
         acc_pool = pools.enter_context(tc.psum_pool(name="acc", bufs=2))
 
         ident = keep.tile([P, P], BF16)
-        make_identity(nc, ident[:])
-
-        r_raw = stage.tile([P, R_COLS], BF16)
-        for rep in range(4):
-            nc.scalar.dma_start(out=r_raw[32 * rep : 32 * rep + 32, R2_AT : R2_AT + 32], in_=R2[:, :])
-        for rep in range(2):
-            nc.scalar.dma_start(out=r_raw[64 * rep : 64 * rep + 64, R0_AT : R0_AT + 64], in_=R0[:, :])
-        nc.scalar.dma_start(out=r_raw[:, R1_AT : R1_AT + 128], in_=R1[:, :])
-        l2_raw = stage.tile([P, 32, 128], BF16)
-        for rep in range(4):
-            nc.sync.dma_start(
-                out=l2_raw[32 * rep : 32 * rep + 32],
-                in_=L2.rearrange("(a h) n -> h a n", h=4)[rep : rep + 1].to_broadcast([32, 32, 128]),
-            )
-        l0_raw = stage.tile([P, 32, 64], BF16)
-        for rep in range(2):
-            nc.sync.dma_start(
-                out=l0_raw[64 * rep : 64 * rep + 64],
-                in_=L0.rearrange("(a h) n -> h a n", h=2)[rep : rep + 1].to_broadcast([64, 32, 64]),
-            )
-        l1_raw = stage.tile([P, 32, 32], BF16)
-        nc.sync.dma_start(
-            out=l1_raw[:].rearrange("p a n -> p (a n)"),
-            in_=L1.rearrange("a n -> (a n)").partition_broadcast(P),
-        )
-        x_sb = stage.tile([P, TOKEN_TILES, D], BF16)
-        for m in range(TOKEN_TILES):
-            nc.sync.dma_start(out=x_sb[:, m, :], in_=x_rows[m * P : (m + 1) * P, :])
-        bias_all = keep.tile([P, D], BF16)
-        nc.sync.dma_start(out=bias_all[:], in_=bias.partition_broadcast(P))
-
         r_third = keep.tile([P, R_COLS], F32)
-        nc.vector.tensor_scalar_mul(out=r_third[:], in0=r_raw[:], scalar1=1.0 / 3.0)
-
-        def by_cbt(row):
-            return row.rearrange("p (c b t) -> p c b t", c=PASSES, b=B)
-
-        def to_psum(row, name):
-            bank = l_psum.tile([P, ROW], BF16, name=name)
-            for h in range(ROW // MATMUL_COLS):
-                cols = slice(h * MATMUL_COLS, (h + 1) * MATMUL_COLS)
-                nc.tensor.matmul(out=bank[:, cols], lhsT=ident[:], rhs=row[:, cols], start=True, stop=True)
-            return bank
-
         l2_rows = keep.tile([P, 2, 2, ROW], BF16)
-        l2_view = l2_raw[:].rearrange("p (c t) (b f g) -> p g f c b t", t=PACK, f=2, g=2)
         l0_rows = keep.tile([P, 2, ROW], BF16)
-        l0_view = l0_raw[:].rearrange("p (c t) (b f) -> p f c b t", t=PACK, f=2)
         l1_rows = keep.tile([P, ROW], BF16)
-        for f in range(2):
-            nc.vector.tensor_copy(out=by_cbt(l2_rows[:, 0, f, :]), in_=l2_view[:, 0, f])
-        for f in range(2):
-            nc.vector.tensor_copy(out=by_cbt(l0_rows[:, f, :]), in_=l0_view[:, f])
-        nc.vector.tensor_copy(out=by_cbt(l1_rows[:]), in_=l1_raw[:].rearrange("p (c t) b -> p c b t", t=PACK))
-        for f in range(2):
-            nc.vector.tensor_copy(out=by_cbt(l2_rows[:, 1, f, :]), in_=l2_view[:, 1, f])
-        l0_banks = [to_psum(l0_rows[:, f, :], "l0_bank%d" % f) for f in range(2)]
-        l1_bank = to_psum(l1_rows[:], "l1_bank")
+        l0_banks = [l_psum.tile([P, ROW], BF16, name="l0_bank%d" % f) for f in range(2)]
+        l1_bank = l_psum.tile([P, ROW], BF16)
         l1_by_pass = l1_bank[:].rearrange("p (c j) -> p c j", c=PASSES)
-
+        bias_all = keep.tile([P, D], BF16)
         x_codes = keep.tile([P, PASSES * TOKENS], U32, align_bytes=64)
         x_scales = keep.tile([P, PASSES * TOKENS], U8, align_bytes=64)
-        result = keep.tile([P, TOKEN_TILES, D], F32)
 
-        def prepare_x():
+        def load_factors(stage):
+            r_raw = stage.tile([P, R_COLS], BF16)
+            for rep in range(4):
+                nc.scalar.dma_start(out=r_raw[32 * rep : 32 * rep + 32, R2_AT : R2_AT + 32], in_=R2[:, :])
+            for rep in range(2):
+                nc.scalar.dma_start(out=r_raw[64 * rep : 64 * rep + 64, R0_AT : R0_AT + 64], in_=R0[:, :])
+            nc.scalar.dma_start(out=r_raw[:, R1_AT : R1_AT + 128], in_=R1[:, :])
+            l2_raw = stage.tile([P, 32, 128], BF16)
+            for rep in range(4):
+                nc.sync.dma_start(
+                    out=l2_raw[32 * rep : 32 * rep + 32],
+                    in_=L2.rearrange("(a h) n -> h a n", h=4)[rep : rep + 1].to_broadcast([32, 32, 128]),
+                )
+            l0_raw = stage.tile([P, 32, 64], BF16)
+            for rep in range(2):
+                nc.sync.dma_start(
+                    out=l0_raw[64 * rep : 64 * rep + 64],
+                    in_=L0.rearrange("(a h) n -> h a n", h=2)[rep : rep + 1].to_broadcast([64, 32, 64]),
+                )
+            l1_raw = stage.tile([P, 32, 32], BF16)
+            nc.sync.dma_start(
+                out=l1_raw[:].rearrange("p a n -> p (a n)"),
+                in_=L1.rearrange("a n -> (a n)").partition_broadcast(P),
+            )
+            x_sb = stage.tile([P, TOKEN_TILES, D], BF16)
+            for m in range(TOKEN_TILES):
+                nc.sync.dma_start(out=x_sb[:, m, :], in_=x_rows[m * P : (m + 1) * P, :])
+            nc.sync.dma_start(out=bias_all[:], in_=bias.partition_broadcast(P))
+
+            make_identity(nc, ident[:])
+            nc.vector.tensor_scalar_mul(out=r_third[:], in0=r_raw[:], scalar1=1.0 / 3.0)
+
+            def by_cbt(row):
+                return row.rearrange("p (c b t) -> p c b t", c=PASSES, b=B)
+
+            def to_psum(bank, row):
+                for h in range(ROW // MATMUL_COLS):
+                    cols = slice(h * MATMUL_COLS, (h + 1) * MATMUL_COLS)
+                    nc.tensor.matmul(out=bank[:, cols], lhsT=ident[:], rhs=row[:, cols], start=True, stop=True)
+
+            l2_view = l2_raw[:].rearrange("p (c t) (b f g) -> p g f c b t", t=PACK, f=2, g=2)
+            l0_view = l0_raw[:].rearrange("p (c t) (b f) -> p f c b t", t=PACK, f=2)
+            for f in range(2):
+                nc.vector.tensor_copy(out=by_cbt(l2_rows[:, 0, f, :]), in_=l2_view[:, 0, f])
+            for f in range(2):
+                nc.vector.tensor_copy(out=by_cbt(l0_rows[:, f, :]), in_=l0_view[:, f])
+                to_psum(l0_banks[f], l0_rows[:, f, :])
+            nc.vector.tensor_copy(out=by_cbt(l1_rows[:]), in_=l1_raw[:].rearrange("p (c t) b -> p c b t", t=PACK))
+            to_psum(l1_bank, l1_rows[:])
+            for f in range(2):
+                nc.vector.tensor_copy(out=by_cbt(l2_rows[:, 1, f, :]), in_=l2_view[:, 1, f])
+            return x_sb
+
+        def prepare_x(stage, x_sb):
             x_grouped = stage.tile([P, PASSES, TOKENS * PACK], BF16, align_bytes=64)
             for c in range(PASSES):
                 x_t = xt_pool.tile([P, TOKEN_TILES, PACK, P], BF16)
@@ -144,7 +145,7 @@ def tile_klinear_kernel(tc, x, L0, R0, L1, R1, L2, R2, bias, out):
             r0 = r_third[:, R0_AT + 32 * g + d : R0_AT + 32 * g + d + 1]
             partial = partials.tile([P, 2, ROW], F32)
             nc.scalar.activation(out=partial[:], in_=l2_rows[:, g], func=COPY, scale=r2)
-            if (unit * VECTOR_UNITS_OF_8) % 8 < VECTOR_UNITS_OF_8:
+            if q == 0 or ((unit + 1) * VECTOR_UNITS_OF_8) % 8 < VECTOR_UNITS_OF_8:
                 for f in range(2):
                     nc.vector.scalar_tensor_tensor(
                         out=partial[:, f, :],
@@ -186,7 +187,7 @@ def tile_klinear_kernel(tc, x, L0, R0, L1, R1, L2, R2, bias, out):
                 )
             return w_codes, w_scales
 
-        def multiply_block(q, w_codes, w_scales):
+        def multiply_block(result, q, w_codes, w_scales):
             acc = [acc_pool.tile([P, BLOCK_COLS], F32, name="acc%d" % m) for m in range(TOKEN_TILES)]
             for c in range(PASSES):
                 w_cols = slice(c * BLOCK_COLS, (c + 1) * BLOCK_COLS)
@@ -210,12 +211,16 @@ def tile_klinear_kernel(tc, x, L0, R0, L1, R1, L2, R2, bias, out):
                     op=ADD,
                 )
 
-        first = build_block(0)
-        prepare_x()
-        multiply_block(0, *first)
+        with tc.tile_pool(name="stage", bufs=1) as stage:
+            x_sb = load_factors(stage)
+            first = build_block(0)
+            prepare_x(stage, x_sb)
+        late = pools.enter_context(tc.tile_pool(name="late", bufs=1))
+        result = late.tile([P, TOKEN_TILES, D], F32)
+        multiply_block(result, 0, *first)
         for q in range(1, 32 // D_STEP):
             w_codes, w_scales = build_block(q)
-            multiply_block(q, w_codes, w_scales)
+            multiply_block(result, q, w_codes, w_scales)
 
         for m in range(TOKEN_TILES):
             nc.sync.dma_start(out=out_rows[m * P : (m + 1) * P, :], in_=result[:, m, :])

@@ -26,9 +26,9 @@ SLOTS = 4 * D_STEP
 BLOCK_COLS = SLOTS * B
 QUANT_IN = 4096
 MATMUL_COLS = 512
-PARTIAL_BUFS = 8
-PRODUCT_BUFS = 4
-VECTOR_UNITS_OF_8 = 2
+PARTIAL_BUFS = 5
+PRODUCT_BUFS = 3
+VECTOR_UNITS_OF_16 = 5
 
 R2_AT = 0
 R0_AT = 32
@@ -145,7 +145,7 @@ def tile_klinear_kernel(tc, x, L0, R0, L1, R1, L2, R2, bias, out):
             r0 = r_third[:, R0_AT + 32 * g + d : R0_AT + 32 * g + d + 1]
             partial = partials.tile([P, 2, ROW], F32)
             nc.scalar.activation(out=partial[:], in_=l2_rows[:, g], func=COPY, scale=r2)
-            if q == 0 or ((unit + 1) * VECTOR_UNITS_OF_8) % 8 < VECTOR_UNITS_OF_8:
+            if (unit * VECTOR_UNITS_OF_16) % 16 < VECTOR_UNITS_OF_16:
                 for f in range(2):
                     nc.vector.scalar_tensor_tensor(
                         out=partial[:, f, :],
@@ -170,9 +170,11 @@ def tile_klinear_kernel(tc, x, L0, R0, L1, R1, L2, R2, bias, out):
                     op1=ADD,
                 )
 
-        def build_block(q):
+        def build_block(q, finish_earlier_block):
             w_bf16 = blocks.tile([P, PASSES, SLOTS, RUN], BF16, align_bytes=64)
             for e in range(D_STEP):
+                if e == D_STEP // 2:
+                    finish_earlier_block()
                 for g in range(2):
                     build_unit(w_bf16, q, e, g)
             w_codes = blocks.tile([P, PASSES * BLOCK_COLS], U32, align_bytes=64)
@@ -187,7 +189,7 @@ def tile_klinear_kernel(tc, x, L0, R0, L1, R1, L2, R2, bias, out):
                 )
             return w_codes, w_scales
 
-        def multiply_block(result, q, w_codes, w_scales):
+        def multiply_block(w_codes, w_scales):
             acc = [acc_pool.tile([P, BLOCK_COLS], F32, name="acc%d" % m) for m in range(TOKEN_TILES)]
             for c in range(PASSES):
                 w_cols = slice(c * BLOCK_COLS, (c + 1) * BLOCK_COLS)
@@ -202,6 +204,9 @@ def tile_klinear_kernel(tc, x, L0, R0, L1, R1, L2, R2, bias, out):
                         start=(c == 0),
                         stop=(c == PASSES - 1),
                     )
+            return acc
+
+        def finish_block(result, q, acc):
             by_n = "p (b s q e) -> p q b s e"
             for m in range(TOKEN_TILES):
                 nc.vector.tensor_tensor(
@@ -213,14 +218,15 @@ def tile_klinear_kernel(tc, x, L0, R0, L1, R1, L2, R2, bias, out):
 
         with tc.tile_pool(name="stage", bufs=1) as stage:
             x_sb = load_factors(stage)
-            first = build_block(0)
+            w_codes, w_scales = build_block(0, lambda: None)
             prepare_x(stage, x_sb)
         late = pools.enter_context(tc.tile_pool(name="late", bufs=1))
         result = late.tile([P, TOKEN_TILES, D], F32)
-        multiply_block(result, 0, *first)
+        acc = multiply_block(w_codes, w_scales)
         for q in range(1, 32 // D_STEP):
-            w_codes, w_scales = build_block(q)
-            multiply_block(result, q, w_codes, w_scales)
+            w_codes, w_scales = build_block(q, lambda: finish_block(result, q - 1, acc))
+            acc = multiply_block(w_codes, w_scales)
+        finish_block(result, 32 // D_STEP - 1, acc)
 
         for m in range(TOKEN_TILES):
             nc.sync.dma_start(out=out_rows[m * P : (m + 1) * P, :], in_=result[:, m, :])

from contextlib import ExitStack

import concourse.mybir as mybir
from concourse.masks import make_identity

F32 = mybir.dt.float32
BF16 = mybir.dt.bfloat16
U32 = mybir.dt.uint32
U8 = mybir.dt.uint8
FP8X4 = mybir.dt.float8_e4m3fn_x4
MULT = mybir.AluOpType.mult
ADD = mybir.AluOpType.add
COPY = mybir.ActivationFunctionType.Copy

P = 128
D = 4096
TOKENS = 256
TOKEN_TILES = TOKENS // P
PACK = 4
PASSES = D // (P * PACK)
B = 32
ROW = PASSES * B * PACK
RUN = B * PACK
D_STEP = 4
SLOTS = 4 * D_STEP
BLOCK_COLS = SLOTS * B
QUANT_IN = 4096
MATMUL_COLS = 512
PARTIAL_BUFS = 5
PRODUCT_BUFS = 3
VECTOR_UNITS_OF_16 = 5

R2_AT = 0
R0_AT = 32
R1_AT = 96
R_COLS = 224

FLOPS = 2 * TOKENS * D * D


def tile_klinear_kernel(tc, x, L0, R0, L1, R1, L2, R2, bias, out):
    nc = tc.nc
    x_rows = x.flatten_outer_dims()
    out_rows = out.flatten_outer_dims()

    with ExitStack() as pools:
        keep = pools.enter_context(tc.tile_pool(name="keep", bufs=1))
        partials = pools.enter_context(tc.tile_pool(name="partials", bufs=PARTIAL_BUFS))
        products = pools.enter_context(tc.tile_pool(name="products", bufs=PRODUCT_BUFS))
        blocks = pools.enter_context(tc.tile_pool(name="blocks", bufs=1))
        l_psum = pools.enter_context(tc.psum_pool(name="l_psum", bufs=1))
        xt_pool = pools.enter_context(tc.psum_pool(name="xt", bufs=1))
        acc_pool = pools.enter_context(tc.psum_pool(name="acc", bufs=2))

        ident = keep.tile([P, P], BF16)
        r_third = keep.tile([P, R_COLS], F32)
        l2_rows = keep.tile([P, 2, 2, ROW], BF16)
        l0_rows = keep.tile([P, 2, ROW], BF16)
        l1_rows = keep.tile([P, ROW], BF16)
        l0_banks = [l_psum.tile([P, ROW], BF16, name="l0_bank%d" % f) for f in range(2)]
        l1_bank = l_psum.tile([P, ROW], BF16)
        l1_by_pass = l1_bank[:].rearrange("p (c j) -> p c j", c=PASSES)
        bias_all = keep.tile([P, D], BF16)
        x_codes = keep.tile([P, PASSES * TOKENS], U32, align_bytes=64)
        x_scales = keep.tile([P, PASSES * TOKENS], U8, align_bytes=64)

        def load_factors(stage):
            r_raw = stage.tile([P, R_COLS], BF16)
            for rep in range(4):
                nc.scalar.dma_start(out=r_raw[32 * rep : 32 * rep + 32, R2_AT : R2_AT + 32], in_=R2[:, :])
            for rep in range(2):
                nc.scalar.dma_start(out=r_raw[64 * rep : 64 * rep + 64, R0_AT : R0_AT + 64], in_=R0[:, :])
            nc.scalar.dma_start(out=r_raw[:, R1_AT : R1_AT + 128], in_=R1[:, :])
            l2_raw = stage.tile([P, 32, 128], BF16)
            for rep in range(4):
                nc.sync.dma_start(
                    out=l2_raw[32 * rep : 32 * rep + 32],
                    in_=L2.rearrange("(a h) n -> h a n", h=4)[rep : rep + 1].to_broadcast([32, 32, 128]),
                )
            l0_raw = stage.tile([P, 32, 64], BF16)
            for rep in range(2):
                nc.sync.dma_start(
                    out=l0_raw[64 * rep : 64 * rep + 64],
                    in_=L0.rearrange("(a h) n -> h a n", h=2)[rep : rep + 1].to_broadcast([64, 32, 64]),
                )
            l1_raw = stage.tile([P, 32, 32], BF16)
            nc.sync.dma_start(
                out=l1_raw[:].rearrange("p a n -> p (a n)"),
                in_=L1.rearrange("a n -> (a n)").partition_broadcast(P),
            )
            x_sb = stage.tile([P, TOKEN_TILES, D], BF16)
            for m in range(TOKEN_TILES):
                nc.sync.dma_start(out=x_sb[:, m, :], in_=x_rows[m * P : (m + 1) * P, :])
            nc.sync.dma_start(out=bias_all[:], in_=bias.partition_broadcast(P))

            make_identity(nc, ident[:])
            nc.vector.tensor_scalar_mul(out=r_third[:], in0=r_raw[:], scalar1=1.0 / 3.0)

            def by_cbt(row):
                return row.rearrange("p (c b t) -> p c b t", c=PASSES, b=B)

            def to_psum(bank, row):
                for h in range(ROW // MATMUL_COLS):
                    cols = slice(h * MATMUL_COLS, (h + 1) * MATMUL_COLS)
                    nc.tensor.matmul(out=bank[:, cols], lhsT=ident[:], rhs=row[:, cols], start=True, stop=True)

            l2_view = l2_raw[:].rearrange("p (c t) (b f g) -> p g f c b t", t=PACK, f=2, g=2)
            l0_view = l0_raw[:].rearrange("p (c t) (b f) -> p f c b t", t=PACK, f=2)
            for f in range(2):
                nc.vector.tensor_copy(out=by_cbt(l2_rows[:, 0, f, :]), in_=l2_view[:, 0, f])
            for f in range(2):
                nc.vector.tensor_copy(out=by_cbt(l0_rows[:, f, :]), in_=l0_view[:, f])
                to_psum(l0_banks[f], l0_rows[:, f, :])
            nc.vector.tensor_copy(out=by_cbt(l1_rows[:]), in_=l1_raw[:].rearrange("p (c t) b -> p c b t", t=PACK))
            to_psum(l1_bank, l1_rows[:])
            for f in range(2):
                nc.vector.tensor_copy(out=by_cbt(l2_rows[:, 1, f, :]), in_=l2_view[:, 1, f])
            return x_sb

        def prepare_x(stage, x_sb):
            x_grouped = stage.tile([P, PASSES, TOKENS * PACK], BF16, align_bytes=64)
            for c in range(PASSES):
                x_t = xt_pool.tile([P, TOKEN_TILES, PACK, P], BF16)
                for m in range(TOKEN_TILES):
                    for t in range(PACK):
                        k0 = (c * PACK + t) * P
                        nc.tensor.transpose(x_t[:, m, t, :], x_sb[:, m, k0 : k0 + P], ident[:])
                nc.scalar.copy(
                    out=x_grouped[:, c, :].rearrange("p (m r t) -> p m r t", m=TOKEN_TILES, t=PACK),
                    in_=x_t[:].rearrange("p m t r -> p m r t"),
                )
            x_flat = x_grouped[:].rearrange("p c j -> p (c j)")
            for h in range(PASSES * TOKENS * PACK // QUANT_IN):
                words = slice(h * QUANT_IN // PACK, (h + 1) * QUANT_IN // PACK)
                nc.vector.quantize_mx(
                    out=x_codes[:, words].bitcast(FP8X4),
                    scales=x_scales[:, words],
                    in_=x_flat[:, h * QUANT_IN : (h + 1) * QUANT_IN],
                )

        def build_unit(w_bf16, q, e, g):
            d = D_STEP * q + e
            unit = 2 * d + g
            r2 = r_third[:, R2_AT + d : R2_AT + d + 1]
            r0 = r_third[:, R0_AT + 32 * g + d : R0_AT + 32 * g + d + 1]
            partial = partials.tile([P, 2, ROW], F32)
            nc.scalar.activation(out=partial[:], in_=l2_rows[:, g], func=COPY, scale=r2)
            if (unit * VECTOR_UNITS_OF_16) % 16 < VECTOR_UNITS_OF_16:
                for f in range(2):
                    nc.vector.scalar_tensor_tensor(
                        out=partial[:, f, :],
                        in0=l0_banks[f][:],
                        scalar=r0,
                        in1=partial[:, f, :],
                        op0=MULT,
                        op1=ADD,
                    )
            else:
                product = products.tile([P, 2, ROW], F32)
                nc.scalar.activation(out=product[:], in_=l0_rows[:], func=COPY, scale=r0)
                nc.gpsimd.tensor_tensor(out=partial[:], in0=partial[:], in1=product[:], op=ADD)
            for f in range(2):
                r1_at = R1_AT + 64 * f + 32 * g + d
                nc.vector.scalar_tensor_tensor(
                    out=w_bf16[:, :, (2 * f + g) * D_STEP + e, :],
                    in0=l1_by_pass,
                    scalar=r_third[:, r1_at : r1_at + 1],
                    in1=partial[:, f, :].rearrange("p (c j) -> p c j", c=PASSES),
                    op0=MULT,
                    op1=ADD,
                )

        def build_block(q, finish_earlier_block):
            w_bf16 = blocks.tile([P, PASSES, SLOTS, RUN], BF16, align_bytes=64)
            for e in range(D_STEP):
                if e == D_STEP // 2:
                    finish_earlier_block()
                for g in range(2):
                    build_unit(w_bf16, q, e, g)
            w_codes = blocks.tile([P, PASSES * BLOCK_COLS], U32, align_bytes=64)
            w_scales = blocks.tile([P, PASSES * BLOCK_COLS], U8, align_bytes=64)
            w_flat = w_bf16[:].rearrange("p c s j -> p (c s j)")
            for h in range(PASSES * BLOCK_COLS * PACK // QUANT_IN):
                words = slice(h * QUANT_IN // PACK, (h + 1) * QUANT_IN // PACK)
                nc.vector.quantize_mx(
                    out=w_codes[:, words].bitcast(FP8X4),
                    scales=w_scales[:, words],
                    in_=w_flat[:, h * QUANT_IN : (h + 1) * QUANT_IN],
                )
            return w_codes, w_scales

        def multiply_block(w_codes, w_scales):
            acc = [acc_pool.tile([P, BLOCK_COLS], F32, name="acc%d" % m) for m in range(TOKEN_TILES)]
            for c in range(PASSES):
                w_cols = slice(c * BLOCK_COLS, (c + 1) * BLOCK_COLS)
                for m in range(TOKEN_TILES):
                    x_cols = slice(c * TOKENS + m * P, c * TOKENS + (m + 1) * P)
                    nc.tensor.matmul_mx(
                        out=acc[m][:],
                        lhsT=x_codes[:, x_cols].bitcast(FP8X4),
                        lhsT_scale=x_scales[:, x_cols],
                        rhs=w_codes[:, w_cols].bitcast(FP8X4),
                        rhs_scale=w_scales[:, w_cols],
                        start=(c == 0),
                        stop=(c == PASSES - 1),
                    )
            return acc

        def finish_block(result, q, acc):
            by_n = "p (b s q e) -> p q b s e"
            for m in range(TOKEN_TILES):
                nc.vector.tensor_tensor(
                    out=result[:, m, :].rearrange(by_n, b=B, s=4, e=D_STEP)[:, q],
                    in0=acc[m][:].rearrange("p (s e b) -> p b s e", s=4, e=D_STEP),
                    in1=bias_all[:].rearrange(by_n, b=B, s=4, e=D_STEP)[:, q],
                    op=ADD,
                )

        with tc.tile_pool(name="stage", bufs=1) as stage:
            x_sb = load_factors(stage)
            w_codes, w_scales = build_block(0, lambda: None)
            prepare_x(stage, x_sb)
        late = pools.enter_context(tc.tile_pool(name="late", bufs=1))
        result = late.tile([P, TOKEN_TILES, D], F32)
        acc = multiply_block(w_codes, w_scales)
        for q in range(1, 32 // D_STEP):
            w_codes, w_scales = build_block(q, lambda: finish_block(result, q - 1, acc))
            acc = multiply_block(w_codes, w_scales)
        finish_block(result, 32 // D_STEP - 1, acc)

        for m in range(TOKEN_TILES):
            nc.sync.dma_start(out=out_rows[m * P : (m + 1) * P, :], in_=result[:, m, :])
